import numpy as np
import ml_dtypes


def mxq(x, axis, fmt="e4m3"):
    dtype, down = {"e4m3": (ml_dtypes.float8_e4m3fn, 7), "e5m2": (ml_dtypes.float8_e5m2, 14)}[fmt]
    v = np.moveaxis(np.asarray(x, np.float32).astype(ml_dtypes.bfloat16).astype(np.float64), axis, -1)
    blocks = v.reshape(v.shape[:-1] + (-1, 32))
    amax = np.abs(blocks).max(-1, keepdims=True)
    byte = np.maximum(np.where(amax > 0, np.frexp(amax)[1] - 1 + 127, 0) - down, 1)
    scale = np.exp2(byte - 127.0)
    codes = (blocks / scale).astype(np.float32).astype(dtype).astype(np.float64)
    return np.moveaxis((codes * scale).reshape(v.shape), -1, axis)


WIDE = False


def mx_kscale(k):
    if not WIDE:
        return np.ones(k)
    levels = np.array([10, -10, 5, -5, 0])
    a = np.random.permutation(np.resize(levels, k // 512 * 4)).reshape(k // 512, 4)
    idx = np.arange(k)
    return np.exp2(a[idx // 512, idx % 128 // 32])


BF16 = ml_dtypes.bfloat16


def bf(x):
    return np.asarray(x, np.float32).astype(BF16)


def f64(x):
    return np.asarray(x).astype(np.float64)


E2M1 = np.array([0.0, 0.5, 1.0, 1.5, 2.0, 3.0, 4.0, 6.0, -0.0, -0.5, -1.0, -1.5, -2.0, -3.0, -4.0, -6.0])


def pack_weight(w, fmt):
    k, n = w.shape
    w = f64(bf(w)).reshape(k // 32, 32, n)
    amax = np.abs(w).max(1)
    if fmt == "e4m3":
        byte = np.frexp(amax)[1] - 1 + 127 - 7
    else:
        mant, ex = np.frexp(amax / 6.0)
        byte = np.where(mant > 0.5, ex, ex - 1) + 127
    byte = np.clip(np.where(amax > 0, byte, 1), 1, 254)
    scaled = (w * np.exp2(127.0 - byte)[:, None, :]).reshape(k, n).astype(np.float32)
    by_word = np.ascontiguousarray(scaled.reshape(k // 512, 128, 4, n).transpose(0, 1, 3, 2))
    if fmt == "e4m3":
        words = by_word.astype(ml_dtypes.float8_e4m3fn).view(np.uint8)
    else:
        c = by_word.astype(ml_dtypes.float4_e2m1fn).view(np.uint8) & 0xF
        words = c[..., 0::2] | (c[..., 1::2] << 4)
    return np.ascontiguousarray(words), np.ascontiguousarray(byte.astype(np.uint8).reshape(k // 512, 16, n))


def unpack_weight(words, scales, fmt):
    g, p, n, _ = words.shape
    if fmt == "e4m3":
        vals = np.ascontiguousarray(words).view(ml_dtypes.float8_e4m3fn).astype(np.float64)
    else:
        nib = np.empty((g, p, n, 4), np.uint8)
        nib[..., 0::2] = words & 0xF
        nib[..., 1::2] = words >> 4
        vals = E2M1[nib]
    vals = vals * np.repeat(np.exp2(scales.astype(np.float64) - 127.0), 8, axis=1)[..., None]
    return vals.transpose(0, 1, 3, 2).reshape(g * 512, n)


B, NE, D, H = 2, 512, 1024, 16
HD = D // H
LN_EPS = 1e-5
FMT = "e4m3"


def setup_inputs():
    s = mx_kscale(D)
    r = np.exp2(-8.0 * np.random.random_sample((B, NE, 1)))
    inp = bf((np.random.standard_normal((B, NE, D)) + 0.5) * r)
    gamma = bf((1.0 + 0.1 * np.random.standard_normal(D)) * s)
    beta = bf(0.1 * np.random.standard_normal(D) * s)
    W_qk_words, W_qk_scales = pack_weight(np.random.standard_normal((D, 2 * D)) / np.sqrt(D) / s[:, None], FMT)
    b_qk = bf(0.1 * np.random.standard_normal(2 * D))
    W_v_words, W_v_scales = pack_weight(np.random.standard_normal((D, D)) / np.sqrt(D) / s[:, None], FMT)
    b_v = bf(0.1 * np.random.standard_normal(D))
    return {
        "inp": inp,
        "gamma": gamma,
        "beta": beta,
        "W_qk_words": W_qk_words,
        "W_qk_scales": W_qk_scales,
        "b_qk": b_qk,
        "W_v_words": W_v_words,
        "W_v_scales": W_v_scales,
        "b_v": b_v,
    }


def reference(inp, gamma, beta, W_qk_words, W_qk_scales, b_qk, W_v_words, W_v_scales, b_v):
    inp = f64(inp)
    mu = np.mean(inp, axis=-1, keepdims=True)
    var = np.mean(np.square(inp - mu), axis=-1, keepdims=True)
    x = (inp - mu) / np.sqrt(var + LN_EPS) * f64(gamma) + f64(beta)
    xq = mxq(x, 2, "e4m3")
    qk = ((xq @ unpack_weight(W_qk_words, W_qk_scales, FMT)) + f64(b_qk)).reshape(B, NE, H, HD, 2)
    q = qk[..., 0]
    k = qk[..., 1]
    v = ((xq @ unpack_weight(W_v_words, W_v_scales, FMT)) + f64(b_v)).reshape(B, NE, H, HD)
    q = np.transpose(q, (0, 2, 1, 3))
    k = np.transpose(k, (0, 2, 3, 1))
    v = np.transpose(v, (0, 2, 1, 3))
    return (q, k, v)

@@ -1,0 +1,287 @@
+from contextlib import ExitStack
+
+import concourse.mybir as mybir
+from concourse.masks import make_identity
+
+F32 = mybir.dt.float32
+BF16 = mybir.dt.bfloat16
+I32 = mybir.dt.int32
+U8 = mybir.dt.uint8
+FP8X4 = mybir.dt.float8_e4m3fn_x4
+ACT = mybir.ActivationFunctionType
+ALU = mybir.AluOpType
+
+P = 128
+PACK = 4
+K_PASS = P * PACK
+N_TILE = 512
+
+B, NE, D, H, HD = 2, 512, 1024, 16, 64
+LN_EPS = 1e-5
+M_TILES = NE // P
+G = D // K_PASS
+QK_TILES = 2 * D // N_TILE
+V_TILES = D // N_TILE
+BN_CHUNK = 512
+BN_STATS = 6
+
+FLOPS = 2 * B * NE * D * 3 * D
+
+
+def tile_relational_kernel(
+    tc, inp, gamma, beta, W_qk_words, W_qk_scales, b_qk, W_v_words, W_v_scales, b_v, out_0, out_1, out_2
+):
+    nc = tc.nc
+    with ExitStack() as ctx:
+        consts = ctx.enter_context(tc.tile_pool(name="consts", bufs=1))
+        batch = ctx.enter_context(tc.tile_pool(name="batch", bufs=B))
+        small = ctx.enter_context(tc.tile_pool(name="small", bufs=4))
+        results = ctx.enter_context(tc.tile_pool(name="results", bufs=3))
+        acc_pool = ctx.enter_context(tc.psum_pool(name="acc", bufs=4))
+        xt_pool = ctx.enter_context(tc.psum_pool(name="xt", bufs=2))
+        kt_pool = ctx.enter_context(tc.psum_pool(name="kt", bufs=2))
+
+        x_in = []
+        for b in range(B):
+            x_in.append(batch.tile([P, M_TILES, D], BF16, name="x_in"))
+
+        def load_rows(b):
+            rows = inp[b].rearrange("(p m) d -> p m d", m=M_TILES)
+            for m in range(M_TILES):
+                nc.sync.dma_start(out=x_in[b][:, m, :], in_=rows[:, m, :])
+
+        load_rows(0)
+
+        w_planes = consts.tile([P, 2 * D], U8, align_bytes=64)
+        nc.vector.memset(w_planes[:].bitcast(I32), 0)
+        for quad in range(4):
+            nc.sync.dma_start(
+                out=w_planes[32 * quad : 32 * quad + 8, :].bitcast(I32),
+                in_=W_qk_scales[:, 4 * quad : 4 * quad + 4, :].bitcast(I32),
+            )
+            nc.sync.dma_start(
+                out=w_planes[32 * quad + 8 : 32 * quad + 16, 0:D].bitcast(I32),
+                in_=W_v_scales[:, 4 * quad : 4 * quad + 4, :].bitcast(I32),
+            )
+
+        wqk_words = consts.tile([P, G, 2 * D], I32, align_bytes=64)
+        wv_words = consts.tile([P, G, D], I32, align_bytes=64)
+        for g in range(G):
+            nc.sync.dma_start(
+                out=wqk_words[:, g, :], in_=W_qk_words[g].rearrange("p n t -> p (n t)").bitcast(I32)
+            )
+        load_rows(1)
+        for g in range(G):
+            nc.sync.dma_start(
+                out=wv_words[:, g, :], in_=W_v_words[g].rearrange("p n t -> p (n t)").bitcast(I32)
+            )
+
+        gamma_bf = consts.tile([P, G, PACK], BF16)
+        beta_bf = consts.tile([P, G, PACK], BF16)
+        bqk_bf = consts.tile([P, QK_TILES, PACK], BF16)
+        nc.scalar.dma_start(out=gamma_bf[:], in_=gamma.rearrange("(g p t) -> p g t", g=G, t=PACK))
+        nc.scalar.dma_start(out=beta_bf[:], in_=beta.rearrange("(g p t) -> p g t", g=G, t=PACK))
+        nc.scalar.dma_start(out=bqk_bf[:], in_=b_qk.rearrange("(n p t) -> p n t", n=QK_TILES, t=PACK))
+        gamma_col = consts.tile([P, G * PACK], F32)
+        beta_col = consts.tile([P, G * PACK], F32)
+        bk_col = consts.tile([P, QK_TILES, 2], F32)
+        nc.vector.tensor_copy(out=gamma_col[:], in_=gamma_bf[:].rearrange("p g t -> p (g t)"))
+        nc.vector.tensor_copy(out=beta_col[:], in_=beta_bf[:].rearrange("p g t -> p (g t)"))
+        nc.vector.tensor_copy(out=bk_col[:], in_=bqk_bf[:].rearrange("p n (c e) -> p n c e", e=2)[:, :, :, 1])
+
+        bias_rows = consts.tile([P, 3 * D], BF16)
+        nc.vector.memset(bias_rows[:].bitcast(I32), 0)
+        nc.scalar.dma_start(out=bias_rows[0:1, 0 : 2 * D], in_=b_qk.unsqueeze(0))
+        nc.scalar.dma_start(out=bias_rows[0:1, 2 * D : 3 * D], in_=b_v.unsqueeze(0))
+        ones = consts.tile([P, P], BF16)
+        nc.vector.memset(ones[:], 1.0)
+        bias_q = consts.tile([P, D], F32)
+        bias_v = consts.tile([P, D], F32)
+        for n in range(QK_TILES):
+            spread = acc_pool.tile([P, N_TILE], F32, name="acc")
+            nc.tensor.matmul(
+                out=spread[:], lhsT=ones[:], rhs=bias_rows[:, n * N_TILE : (n + 1) * N_TILE], start=True, stop=True
+            )
+            nc.scalar.copy(
+                out=bias_q[:, n * N_TILE // 2 : (n + 1) * N_TILE // 2],
+                in_=spread[:].rearrange("p (f e) -> p f e", e=2)[:, :, 0],
+            )
+        for n in range(V_TILES):
+            spread = acc_pool.tile([P, N_TILE], F32, name="acc")
+            nc.tensor.matmul(
+                out=spread[:],
+                lhsT=ones[:],
+                rhs=bias_rows[:, 2 * D + n * N_TILE : 2 * D + (n + 1) * N_TILE],
+                start=True,
+                stop=True,
+            )
+            nc.scalar.copy(out=bias_v[:, n * N_TILE : (n + 1) * N_TILE], in_=spread[:])
+
+        ident = consts.tile([P, P], F32)
+        make_identity(nc, ident[:])
+
+        y, x_planes, x_grouped, x_codes, x_scales = [], [], [], [], []
+        for b in range(B):
+            y.append(batch.tile([P, M_TILES, G, PACK, P], F32, name="y"))
+            x_planes.append(batch.tile([P, G, PACK, NE], BF16, name="x_planes"))
+            x_grouped.append(batch.tile([P, G, NE, PACK], BF16, name="x_grouped", align_bytes=64))
+            x_codes.append(batch.tile([P, G, NE], I32, name="x_codes", align_bytes=64))
+            x_scales.append(batch.tile([P, G, NE], U8, name="x_scales", align_bytes=64))
+
+        def normalise_rows(b, m):
+            rows = x_in[b][:, m, :]
+            stats = small.tile([P, D // BN_CHUNK, BN_STATS], F32, name="stats")
+            for s in range(D // BN_CHUNK):
+                nc.vector.bn_stats(out=stats[:, s, :], in_=rows[:, s * BN_CHUNK : (s + 1) * BN_CHUNK])
+            mean_var = small.tile([P, 2], F32, name="mean_var")
+            nc.vector.bn_aggr(out=mean_var[:], in_=stats[:].rearrange("p s k -> p (s k)"))
+            var_eps = small.tile([P, 1], F32, name="var_eps")
+            nc.vector.tensor_scalar(out=var_eps[:], in0=mean_var[:, 1:2], scalar1=LN_EPS, scalar2=None, op0=ALU.add)
+            std = small.tile([P, 1], F32, name="std")
+            nc.scalar.activation(out=std[:], in_=var_eps[:], func=ACT.Sqrt)
+            rstd = small.tile([P, 1], F32, name="rstd")
+            nc.vector.reciprocal(out=rstd[:], in_=std[:])
+            shift = small.tile([P, 1], F32, name="shift")
+            nc.vector.tensor_scalar(
+                out=shift[:], in0=mean_var[:, 0:1], scalar1=rstd[:, 0:1], scalar2=-1.0, op0=ALU.mult, op1=ALU.mult
+            )
+            nc.scalar.activation(
+                out=y[b][:, m],
+                in_=rows.rearrange("p (g q t) -> p g t q", g=G, t=PACK),
+                func=ACT.Identity,
+                scale=rstd[:, 0:1],
+                bias=shift[:, 0:1],
+            )
+
+        def transpose_pass(b, g):
+            for t in range(PACK):
+                xt = xt_pool.tile([P, M_TILES, P], F32, name="xt")
+                for m in range(M_TILES):
+                    nc.tensor.transpose(out=xt[:, m, :], in_=y[b][:, m, g, t, :], identity=ident[:])
+                col = g * PACK + t
+                if t % 2 == 0:
+                    nc.scalar.activation(
+                        out=x_planes[b][:, g, t, :],
+                        in_=xt[:].rearrange("p m n -> p (m n)"),
+                        func=ACT.Identity,
+                        scale=gamma_col[:, col : col + 1],
+                        bias=beta_col[:, col : col + 1],
+                    )
+                else:
+                    nc.vector.tensor_scalar(
+                        out=x_planes[b][:, g, t, :],
+                        in0=xt[:].rearrange("p m n -> p (m n)"),
+                        scalar1=gamma_col[:, col : col + 1],
+                        scalar2=beta_col[:, col : col + 1],
+                        op0=ALU.mult,
+                        op1=ALU.add,
+                    )
+
+        def group_pass(b, g):
+            nc.vector.tensor_copy(
+                out=x_grouped[b][:, g].rearrange("p (c i) t -> p c t i", i=4),
+                in_=x_planes[b][:, g].rearrange("p t (c i) -> p c t i", i=4),
+            )
+
+        def quantise_pass(b, g):
+            nc.vector.quantize_mx(
+                out=x_codes[b][:, g, :].bitcast(FP8X4),
+                scales=x_scales[b][:, g, :],
+                in_=x_grouped[b][:, g].rearrange("p c t -> p (c t)"),
+            )
+
+        def product(b, m, words, plane_start, cols):
+            acc = acc_pool.tile([P, N_TILE], F32, name="acc")
+            for g in range(G):
+                nc.tensor.matmul_mx(
+                    out=acc[:],
+                    lhsT=x_codes[b][:, g, m * P : (m + 1) * P].bitcast(FP8X4),
+                    lhsT_scale=x_scales[b][:, g, m * P : (m + 1) * P],
+                    rhs=words[:, g, cols].bitcast(FP8X4),
+                    rhs_scale=w_planes[plane_start + PACK * g : P, cols],
+                    start=(g == 0),
+                    stop=(g == G - 1),
+                )
+            return acc
+
+        k_rows = {}
+
+        def project_qk(b, n):
+            cols = slice(n * N_TILE, (n + 1) * N_TILE)
+            q_sb = results.tile([P, 4, M_TILES, HD], F32, name="q_sb")
+            k_rows[(b, n)] = results.tile([P, M_TILES, 2, P], F32, name="k_rows")
+            for m in range(M_TILES):
+                acc = product(b, m, wqk_words, 0, cols)
+                nc.vector.tensor_tensor(
+                    out=q_sb[:, :, m, :],
+                    in0=acc[:].rearrange("p (h j e) -> p h j e", h=4, e=2)[:, :, :, 0],
+                    in1=bias_q[:, n * N_TILE // 2 : (n + 1) * N_TILE // 2].rearrange("p (h j) -> p h j", h=4),
+                    op=ALU.add,
+                )
+                nc.scalar.copy(
+                    out=k_rows[(b, n)][:, m],
+                    in_=acc[:].rearrange("p (f c e) -> p c f e", c=2, e=2)[:, :, :, 1],
+                )
+            nc.sync.dma_start(
+                out=out_0[b, 4 * n : 4 * n + 4].rearrange("h (p m) j -> p h (m j)", m=M_TILES),
+                in_=q_sb[:].rearrange("p h m j -> p h (m j)"),
+            )
+
+        def transpose_k(b, n):
+            k_sb = results.tile([P, 2, NE], F32, name="k_sb")
+            for c in range(2):
+                kt = kt_pool.tile([P, M_TILES, P], F32, name="kt")
+                for m in range(M_TILES):
+                    nc.tensor.transpose(out=kt[:, m, :], in_=k_rows[(b, n)][:, m, c, :], identity=ident[:])
+                nc.scalar.activation(
+                    out=k_sb[:, c, :].rearrange("f (p m) -> f p m", m=M_TILES),
+                    in_=kt[:].rearrange("f m p -> f p m"),
+                    func=ACT.Identity,
+                    bias=bk_col[:, n, c : c + 1],
+                )
+            features = out_1[b].rearrange("h j r -> (h j) r")[2 * P * n : 2 * P * (n + 1), :]
+            nc.sync.dma_start(
+                out=features.rearrange("(f c) r -> f (c r)", c=2), in_=k_sb[:].rearrange("f c r -> f (c r)")
+            )
+
+        def project_v(b, n):
+            cols = slice(n * N_TILE, (n + 1) * N_TILE)
+            v_sb = results.tile([P, 8, M_TILES, HD], F32, name="v_sb")
+            for m in range(M_TILES):
+                acc = product(b, m, wv_words, 2 * PACK, cols)
+                nc.vector.tensor_tensor(
+                    out=v_sb[:, :, m, :],
+                    in0=acc[:].rearrange("p (h j) -> p h j", h=8),
+                    in1=bias_v[:, cols].rearrange("p (h j) -> p h j", h=8),
+                    op=ALU.add,
+                )
+            nc.sync.dma_start(
+                out=out_2[b, 8 * n : 8 * n + 8].rearrange("h (p m) j -> p h (m j)", m=M_TILES),
+                in_=v_sb[:].rearrange("p h m j -> p h (m j)"),
+            )
+
+        def prepare(b, step):
+            if step < 2:
+                normalise_rows(b, 2 * step)
+                normalise_rows(b, 2 * step + 1)
+            elif step < 4:
+                transpose_pass(b, step - 2)
+                group_pass(b, step - 2)
+            if step == 3:
+                for g in range(G):
+                    quantise_pass(b, g)
+
+        for step in range(4):
+            prepare(0, step)
+
+        for b in range(B):
+            for half in range(2):
+                project_qk(b, 2 * half)
+                if b + 1 < B:
+                    prepare(b + 1, 2 * half)
+                project_qk(b, 2 * half + 1)
+                transpose_k(b, 2 * half)
+                if b + 1 < B:
+                    prepare(b + 1, 2 * half + 1)
+                project_v(b, half)
+                transpose_k(b, 2 * half + 1)

@@ -15,8 +15,9 @@ P = 128
 PACK = 4
 K_PASS = P * PACK
 N_TILE = 512
+PSUM_BANKS = 8
 
-B, NE, D, H, HD = 2, 512, 1024, 16, 64
+B, NE, D, HD = 2, 512, 1024, 64
 LN_EPS = 1e-5
 M_TILES = NE // P
 G = D // K_PASS
@@ -24,6 +25,7 @@ QK_TILES = 2 * D // N_TILE
 V_TILES = D // N_TILE
 BN_CHUNK = 512
 BN_STATS = 6
+EARLY_TILES = 6
 
 FLOPS = 2 * B * NE * D * 3 * D
 
@@ -33,24 +35,19 @@ def tile_relational_kernel(
 ):
     nc = tc.nc
     with ExitStack() as ctx:
+        ctx.enter_context(tc.manual_schedule())
         consts = ctx.enter_context(tc.tile_pool(name="consts", bufs=1))
         batch = ctx.enter_context(tc.tile_pool(name="batch", bufs=B))
-        small = ctx.enter_context(tc.tile_pool(name="small", bufs=4))
+        small = ctx.enter_context(tc.tile_pool(name="small", bufs=8))
         results = ctx.enter_context(tc.tile_pool(name="results", bufs=3))
-        acc_pool = ctx.enter_context(tc.psum_pool(name="acc", bufs=4))
-        xt_pool = ctx.enter_context(tc.psum_pool(name="xt", bufs=2))
-        kt_pool = ctx.enter_context(tc.psum_pool(name="kt", bufs=2))
+        psum = ctx.enter_context(tc.psum_pool(name="psum", bufs=PSUM_BANKS))
 
         x_in = []
         for b in range(B):
             x_in.append(batch.tile([P, M_TILES, D], BF16, name="x_in"))
-
-        def load_rows(b):
             rows = inp[b].rearrange("(p m) d -> p m d", m=M_TILES)
             for m in range(M_TILES):
                 nc.sync.dma_start(out=x_in[b][:, m, :], in_=rows[:, m, :])
-
-        load_rows(0)
 
         w_planes = consts.tile([P, 2 * D], U8, align_bytes=64)
         nc.vector.memset(w_planes[:].bitcast(I32), 0)
@@ -70,7 +67,6 @@ def tile_relational_kernel(
             nc.sync.dma_start(
                 out=wqk_words[:, g, :], in_=W_qk_words[g].rearrange("p n t -> p (n t)").bitcast(I32)
             )
-        load_rows(1)
         for g in range(G):
             nc.sync.dma_start(
                 out=wv_words[:, g, :], in_=W_v_words[g].rearrange("p n t -> p (n t)").bitcast(I32)
@@ -82,12 +78,6 @@ def tile_relational_kernel(
         nc.scalar.dma_start(out=gamma_bf[:], in_=gamma.rearrange("(g p t) -> p g t", g=G, t=PACK))
         nc.scalar.dma_start(out=beta_bf[:], in_=beta.rearrange("(g p t) -> p g t", g=G, t=PACK))
         nc.scalar.dma_start(out=bqk_bf[:], in_=b_qk.rearrange("(n p t) -> p n t", n=QK_TILES, t=PACK))
-        gamma_col = consts.tile([P, G * PACK], F32)
-        beta_col = consts.tile([P, G * PACK], F32)
-        bk_col = consts.tile([P, QK_TILES, 2], F32)
-        nc.vector.tensor_copy(out=gamma_col[:], in_=gamma_bf[:].rearrange("p g t -> p (g t)"))
-        nc.vector.tensor_copy(out=beta_col[:], in_=beta_bf[:].rearrange("p g t -> p (g t)"))
-        nc.vector.tensor_copy(out=bk_col[:], in_=bqk_bf[:].rearrange("p n (c e) -> p n c e", e=2)[:, :, :, 1])
 
         bias_rows = consts.tile([P, 3 * D], BF16)
         nc.vector.memset(bias_rows[:].bitcast(I32), 0)
@@ -95,27 +85,10 @@ def tile_relational_kernel(
         nc.scalar.dma_start(out=bias_rows[0:1, 2 * D : 3 * D], in_=b_v.unsqueeze(0))
         ones = consts.tile([P, P], BF16)
         nc.vector.memset(ones[:], 1.0)
-        bias_q = consts.tile([P, D], F32)
-        bias_v = consts.tile([P, D], F32)
-        for n in range(QK_TILES):
-            spread = acc_pool.tile([P, N_TILE], F32, name="acc")
-            nc.tensor.matmul(
-                out=spread[:], lhsT=ones[:], rhs=bias_rows[:, n * N_TILE : (n + 1) * N_TILE], start=True, stop=True
-            )
-            nc.scalar.copy(
-                out=bias_q[:, n * N_TILE // 2 : (n + 1) * N_TILE // 2],
-                in_=spread[:].rearrange("p (f e) -> p f e", e=2)[:, :, 0],
-            )
-        for n in range(V_TILES):
-            spread = acc_pool.tile([P, N_TILE], F32, name="acc")
-            nc.tensor.matmul(
-                out=spread[:],
-                lhsT=ones[:],
-                rhs=bias_rows[:, 2 * D + n * N_TILE : 2 * D + (n + 1) * N_TILE],
-                start=True,
-                stop=True,
-            )
-            nc.scalar.copy(out=bias_v[:, n * N_TILE : (n + 1) * N_TILE], in_=spread[:])
+
+        warm = consts.tile([P, 1], F32)
+        nc.vector.memset(warm[:], 1.0)
+        nc.scalar.activation(out=warm[:], in_=warm[:], func=ACT.Sqrt)
 
         ident = consts.tile([P, P], F32)
         make_identity(nc, ident[:])
@@ -128,41 +101,66 @@ def tile_relational_kernel(
             x_codes.append(batch.tile([P, G, NE], I32, name="x_codes", align_bytes=64))
             x_scales.append(batch.tile([P, G, NE], U8, name="x_scales", align_bytes=64))
 
-        def normalise_rows(b, m):
-            rows = x_in[b][:, m, :]
+        mean_var, std = {}, {}
+
+        def statistics(b, m):
             stats = small.tile([P, D // BN_CHUNK, BN_STATS], F32, name="stats")
             for s in range(D // BN_CHUNK):
-                nc.vector.bn_stats(out=stats[:, s, :], in_=rows[:, s * BN_CHUNK : (s + 1) * BN_CHUNK])
-            mean_var = small.tile([P, 2], F32, name="mean_var")
-            nc.vector.bn_aggr(out=mean_var[:], in_=stats[:].rearrange("p s k -> p (s k)"))
+                nc.vector.bn_stats(out=stats[:, s, :], in_=x_in[b][:, m, s * BN_CHUNK : (s + 1) * BN_CHUNK])
+            mean_var[(b, m)] = small.tile([P, 2], F32, name="mean_var")
+            nc.vector.bn_aggr(out=mean_var[(b, m)][:], in_=stats[:].rearrange("p s k -> p (s k)"))
             var_eps = small.tile([P, 1], F32, name="var_eps")
-            nc.vector.tensor_scalar(out=var_eps[:], in0=mean_var[:, 1:2], scalar1=LN_EPS, scalar2=None, op0=ALU.add)
-            std = small.tile([P, 1], F32, name="std")
-            nc.scalar.activation(out=std[:], in_=var_eps[:], func=ACT.Sqrt)
+            nc.vector.tensor_scalar(
+                out=var_eps[:], in0=mean_var[(b, m)][:, 1:2], scalar1=LN_EPS, scalar2=None, op0=ALU.add
+            )
+            std[(b, m)] = small.tile([P, 1], F32, name="std")
+            nc.scalar.activation(out=std[(b, m)][:], in_=var_eps[:], func=ACT.Sqrt)
+
+        def normalise(b, m):
             rstd = small.tile([P, 1], F32, name="rstd")
-            nc.vector.reciprocal(out=rstd[:], in_=std[:])
+            nc.vector.reciprocal(out=rstd[:], in_=std[(b, m)][:])
             shift = small.tile([P, 1], F32, name="shift")
             nc.vector.tensor_scalar(
-                out=shift[:], in0=mean_var[:, 0:1], scalar1=rstd[:, 0:1], scalar2=-1.0, op0=ALU.mult, op1=ALU.mult
+                out=shift[:],
+                in0=mean_var[(b, m)][:, 0:1],
+                scalar1=rstd[:, 0:1],
+                scalar2=-1.0,
+                op0=ALU.mult,
+                op1=ALU.mult,
             )
-            nc.scalar.activation(
-                out=y[b][:, m],
-                in_=rows.rearrange("p (g q t) -> p g t q", g=G, t=PACK),
-                func=ACT.Identity,
-                scale=rstd[:, 0:1],
-                bias=shift[:, 0:1],
-            )
+            rows = x_in[b][:, m, :].rearrange("p (g q t) -> p g t q", g=G, t=PACK)
+            if b == 0 and m % 2 == 0:
+                nc.scalar.activation(
+                    out=y[b][:, m], in_=rows, func=ACT.Identity, scale=rstd[:, 0:1], bias=shift[:, 0:1]
+                )
+            else:
+                nc.gpsimd.tensor_scalar(
+                    out=y[b][:, m], in0=rows, scalar1=rstd[:, 0:1], scalar2=shift[:, 0:1], op0=ALU.mult, op1=ALU.add
+                )
+
+        def normalise_tiles(first, last):
+            for i in range(first, last):
+                statistics(i // M_TILES, i % M_TILES)
+                if i > 0:
+                    normalise((i - 1) // M_TILES, (i - 1) % M_TILES)
+
+        gamma_col = consts.tile([P, G * PACK], F32)
+        beta_col = consts.tile([P, G * PACK], F32)
+        bk_col = consts.tile([P, QK_TILES, 2], F32)
 
         def transpose_pass(b, g):
+            banks = []
             for t in range(PACK):
-                xt = xt_pool.tile([P, M_TILES, P], F32, name="xt")
-                for m in range(M_TILES):
-                    nc.tensor.transpose(out=xt[:, m, :], in_=y[b][:, m, g, t, :], identity=ident[:])
+                banks.append(psum.tile([P, M_TILES, P], F32, name="bank"))
+            for m in range(M_TILES):
+                for t in range(PACK):
+                    nc.tensor.transpose(out=banks[t][:, m, :], in_=y[b][:, m, g, t, :], identity=ident[:])
+            for t in range(PACK):
                 col = g * PACK + t
                 if t % 2 == 0:
                     nc.scalar.activation(
                         out=x_planes[b][:, g, t, :],
-                        in_=xt[:].rearrange("p m n -> p (m n)"),
+                        in_=banks[t][:].rearrange("p m n -> p (m n)"),
                         func=ACT.Identity,
                         scale=gamma_col[:, col : col + 1],
                         bias=beta_col[:, col : col + 1],
@@ -170,7 +168,7 @@ def tile_relational_kernel(
                 else:
                     nc.vector.tensor_scalar(
                         out=x_planes[b][:, g, t, :],
-                        in0=xt[:].rearrange("p m n -> p (m n)"),
+                        in0=banks[t][:].rearrange("p m n -> p (m n)"),
                         scalar1=gamma_col[:, col : col + 1],
                         scalar2=beta_col[:, col : col + 1],
                         op0=ALU.mult,
@@ -190,8 +188,27 @@ def tile_relational_kernel(
                 in_=x_grouped[b][:, g].rearrange("p c t -> p (c t)"),
             )
 
+        bias_q = consts.tile([P, D], F32)
+        bias_v = consts.tile([P, D], F32)
+
+        def spread_biases():
+            for n in range(QK_TILES + V_TILES):
+                spread = psum.tile([P, N_TILE], F32, name="bank")
+                nc.tensor.matmul(
+                    out=spread[:], lhsT=ones[:], rhs=bias_rows[:, n * N_TILE : (n + 1) * N_TILE], start=True, stop=True
+                )
+                if n < QK_TILES:
+                    nc.scalar.copy(
+                        out=bias_q[:, n * N_TILE // 2 : (n + 1) * N_TILE // 2],
+                        in_=spread[:].rearrange("p (f e) -> p f e", e=2)[:, :, 0],
+                    )
+                else:
+                    nc.scalar.copy(
+                        out=bias_v[:, (n - QK_TILES) * N_TILE : (n - QK_TILES + 1) * N_TILE], in_=spread[:]
+                    )
+
         def product(b, m, words, plane_start, cols):
-            acc = acc_pool.tile([P, N_TILE], F32, name="acc")
+            acc = psum.tile([P, N_TILE], F32, name="bank")
             for g in range(G):
                 nc.tensor.matmul_mx(
                     out=acc[:],
@@ -229,13 +246,15 @@ def tile_relational_kernel(
 
         def transpose_k(b, n):
             k_sb = results.tile([P, 2, NE], F32, name="k_sb")
+            banks = []
             for c in range(2):
-                kt = kt_pool.tile([P, M_TILES, P], F32, name="kt")
+                banks.append(psum.tile([P, M_TILES, P], F32, name="bank"))
                 for m in range(M_TILES):
-                    nc.tensor.transpose(out=kt[:, m, :], in_=k_rows[(b, n)][:, m, c, :], identity=ident[:])
+                    nc.tensor.transpose(out=banks[c][:, m, :], in_=k_rows[(b, n)][:, m, c, :], identity=ident[:])
+            for c in range(2):
                 nc.scalar.activation(
                     out=k_sb[:, c, :].rearrange("f (p m) -> f p m", m=M_TILES),
-                    in_=kt[:].rearrange("f m p -> f p m"),
+                    in_=banks[c][:].rearrange("f m p -> f p m"),
                     func=ACT.Identity,
                     bias=bk_col[:, n, c : c + 1],
                 )
@@ -260,28 +279,39 @@ def tile_relational_kernel(
                 in_=v_sb[:].rearrange("p h m j -> p h (m j)"),
             )
 
-        def prepare(b, step):
-            if step < 2:
-                normalise_rows(b, 2 * step)
-                normalise_rows(b, 2 * step + 1)
-            elif step < 4:
-                transpose_pass(b, step - 2)
-                group_pass(b, step - 2)
-            if step == 3:
-                for g in range(G):
-                    quantise_pass(b, g)
-
-        for step in range(4):
-            prepare(0, step)
+        normalise_tiles(0, EARLY_TILES)
+        nc.vector.tensor_copy(out=gamma_col[:], in_=gamma_bf[:].rearrange("p g t -> p (g t)"))
+        nc.vector.tensor_copy(out=beta_col[:], in_=beta_bf[:].rearrange("p g t -> p (g t)"))
+        nc.vector.tensor_copy(out=bk_col[:], in_=bqk_bf[:].rearrange("p n (c e) -> p n c e", e=2)[:, :, :, 1])
+        transpose_pass(0, 0)
+        group_pass(0, 0)
+        transpose_pass(0, 1)
+        quantise_pass(0, 0)
+        group_pass(0, 1)
+        quantise_pass(0, 1)
+        spread_biases()
+        normalise_tiles(EARLY_TILES, B * M_TILES)
+        normalise(B - 1, M_TILES - 1)
 
         for b in range(B):
-            for half in range(2):
-                project_qk(b, 2 * half)
-                if b + 1 < B:
-                    prepare(b + 1, 2 * half)
-                project_qk(b, 2 * half + 1)
-                transpose_k(b, 2 * half)
-                if b + 1 < B:
-                    prepare(b + 1, 2 * half + 1)
-                project_v(b, half)
-                transpose_k(b, 2 * half + 1)
+            more = b + 1 < B
+            project_qk(b, 0)
+            project_qk(b, 1)
+            transpose_k(b, 0)
+            project_v(b, 0)
+            if more:
+                transpose_pass(b + 1, 0)
+            transpose_k(b, 1)
+            project_qk(b, 2)
+            if more:
+                group_pass(b + 1, 0)
+                transpose_pass(b + 1, 1)
+            project_qk(b, 3)
+            if more:
+                quantise_pass(b + 1, 0)
+            transpose_k(b, 2)
+            if more:
+                group_pass(b + 1, 1)
+                quantise_pass(b + 1, 1)
+            project_v(b, 1)
+            transpose_k(b, 3)

@@ -35,7 +35,6 @@ def tile_relational_kernel(
 ):
     nc = tc.nc
     with ExitStack() as ctx:
-        ctx.enter_context(tc.manual_schedule())
         consts = ctx.enter_context(tc.tile_pool(name="consts", bufs=1))
         batch = ctx.enter_context(tc.tile_pool(name="batch", bufs=B))
         small = ctx.enter_context(tc.tile_pool(name="small", bufs=8))

@@ -78,12 +78,10 @@ def tile_relational_kernel(
         nc.scalar.dma_start(out=beta_bf[:], in_=beta.rearrange("(g p t) -> p g t", g=G, t=PACK))
         nc.scalar.dma_start(out=bqk_bf[:], in_=b_qk.rearrange("(n p t) -> p n t", n=QK_TILES, t=PACK))
 
-        bias_rows = consts.tile([P, 3 * D], BF16)
-        nc.vector.memset(bias_rows[:].bitcast(I32), 0)
-        nc.scalar.dma_start(out=bias_rows[0:1, 0 : 2 * D], in_=b_qk.unsqueeze(0))
-        nc.scalar.dma_start(out=bias_rows[0:1, 2 * D : 3 * D], in_=b_v.unsqueeze(0))
-        ones = consts.tile([P, P], BF16)
-        nc.vector.memset(ones[:], 1.0)
+        bias_qk = consts.tile([P, 2 * D], BF16)
+        bias_v = consts.tile([P, D], BF16)
+        nc.sync.dma_start(out=bias_qk[:], in_=b_qk.partition_broadcast(P))
+        nc.sync.dma_start(out=bias_v[:], in_=b_v.partition_broadcast(P))
 
         warm = consts.tile([P, 1], F32)
         nc.vector.memset(warm[:], 1.0)
@@ -187,25 +185,6 @@ def tile_relational_kernel(
                 in_=x_grouped[b][:, g].rearrange("p c t -> p (c t)"),
             )
 
-        bias_q = consts.tile([P, D], F32)
-        bias_v = consts.tile([P, D], F32)
-
-        def spread_biases():
-            for n in range(QK_TILES + V_TILES):
-                spread = psum.tile([P, N_TILE], F32, name="bank")
-                nc.tensor.matmul(
-                    out=spread[:], lhsT=ones[:], rhs=bias_rows[:, n * N_TILE : (n + 1) * N_TILE], start=True, stop=True
-                )
-                if n < QK_TILES:
-                    nc.scalar.copy(
-                        out=bias_q[:, n * N_TILE // 2 : (n + 1) * N_TILE // 2],
-                        in_=spread[:].rearrange("p (f e) -> p f e", e=2)[:, :, 0],
-                    )
-                else:
-                    nc.scalar.copy(
-                        out=bias_v[:, (n - QK_TILES) * N_TILE : (n - QK_TILES + 1) * N_TILE], in_=spread[:]
-                    )
-
         def product(b, m, words, plane_start, cols):
             acc = psum.tile([P, N_TILE], F32, name="bank")
             for g in range(G):
@@ -231,7 +210,7 @@ def tile_relational_kernel(
                 nc.vector.tensor_tensor(
                     out=q_sb[:, :, m, :],
                     in0=acc[:].rearrange("p (h j e) -> p h j e", h=4, e=2)[:, :, :, 0],
-                    in1=bias_q[:, n * N_TILE // 2 : (n + 1) * N_TILE // 2].rearrange("p (h j) -> p h j", h=4),
+                    in1=bias_qk[:, cols].rearrange("p (h j e) -> p h j e", h=4, e=2)[:, :, :, 0],
                     op=ALU.add,
                 )
                 nc.scalar.copy(
@@ -251,12 +230,21 @@ def tile_relational_kernel(
                 for m in range(M_TILES):
                     nc.tensor.transpose(out=banks[c][:, m, :], in_=k_rows[(b, n)][:, m, c, :], identity=ident[:])
             for c in range(2):
-                nc.scalar.activation(
-                    out=k_sb[:, c, :].rearrange("f (p m) -> f p m", m=M_TILES),
-                    in_=banks[c][:].rearrange("f m p -> f p m"),
-                    func=ACT.Identity,
-                    bias=bk_col[:, n, c : c + 1],
-                )
+                if c == 1 and b == B - 1:
+                    nc.vector.tensor_scalar(
+                        out=k_sb[:, c, :].rearrange("f (p m) -> f p m", m=M_TILES),
+                        in0=banks[c][:].rearrange("f m p -> f p m"),
+                        scalar1=bk_col[:, n, c : c + 1],
+                        scalar2=None,
+                        op0=ALU.add,
+                    )
+                else:
+                    nc.scalar.activation(
+                        out=k_sb[:, c, :].rearrange("f (p m) -> f p m", m=M_TILES),
+                        in_=banks[c][:].rearrange("f m p -> f p m"),
+                        func=ACT.Identity,
+                        bias=bk_col[:, n, c : c + 1],
+                    )
             features = out_1[b].rearrange("h j r -> (h j) r")[2 * P * n : 2 * P * (n + 1), :]
             nc.sync.dma_start(
                 out=features.rearrange("(f c) r -> f (c r)", c=2), in_=k_sb[:].rearrange("f c r -> f (c r)")
@@ -273,10 +261,12 @@ def tile_relational_kernel(
                     in1=bias_v[:, cols].rearrange("p (h j) -> p h j", h=8),
                     op=ALU.add,
                 )
-            nc.sync.dma_start(
-                out=out_2[b, 8 * n : 8 * n + 8].rearrange("h (p m) j -> p h (m j)", m=M_TILES),
-                in_=v_sb[:].rearrange("p h m j -> p h (m j)"),
-            )
+            for half in range(2):
+                heads = slice(4 * half, 4 * half + 4)
+                nc.sync.dma_start(
+                    out=out_2[b, 8 * n : 8 * n + 8][heads].rearrange("h (p m) j -> p h (m j)", m=M_TILES),
+                    in_=v_sb[:, heads].rearrange("p h m j -> p h (m j)"),
+                )
 
         normalise_tiles(0, EARLY_TILES)
         nc.vector.tensor_copy(out=gamma_col[:], in_=gamma_bf[:].rearrange("p g t -> p (g t)"))
@@ -288,7 +278,6 @@ def tile_relational_kernel(
         quantise_pass(0, 0)
         group_pass(0, 1)
         quantise_pass(0, 1)
-        spread_biases()
         normalise_tiles(EARLY_TILES, B * M_TILES)
         normalise(B - 1, M_TILES - 1)
 

@@ -12,8 +12,10 @@ ACT = mybir.ActivationFunctionType
 ALU = mybir.AluOpType
 
 P = 128
+QUADRANT = 32
 PACK = 4
 K_PASS = P * PACK
+PLANE_ROWS = 4
 N_TILE = 512
 PSUM_BANKS = 8
 
@@ -23,9 +25,11 @@ M_TILES = NE // P
 G = D // K_PASS
 QK_TILES = 2 * D // N_TILE
 V_TILES = D // N_TILE
+QK_HEADS = N_TILE // (2 * HD)
+V_HEADS = N_TILE // HD
 BN_CHUNK = 512
 BN_STATS = 6
-EARLY_TILES = 6
+RUN = 4
 
 FLOPS = 2 * B * NE * D * 3 * D
 
@@ -37,8 +41,8 @@ def tile_relational_kernel(
     with ExitStack() as ctx:
         consts = ctx.enter_context(tc.tile_pool(name="consts", bufs=1))
         batch = ctx.enter_context(tc.tile_pool(name="batch", bufs=B))
-        small = ctx.enter_context(tc.tile_pool(name="small", bufs=8))
-        results = ctx.enter_context(tc.tile_pool(name="results", bufs=3))
+        small = ctx.enter_context(tc.tile_pool(name="small", bufs=B * M_TILES))
+        results = ctx.enter_context(tc.tile_pool(name="results", bufs=4))
         psum = ctx.enter_context(tc.psum_pool(name="psum", bufs=PSUM_BANKS))
 
         x_in = []
@@ -50,14 +54,16 @@ def tile_relational_kernel(
 
         w_planes = consts.tile([P, 2 * D], U8, align_bytes=64)
         nc.vector.memset(w_planes[:].bitcast(I32), 0)
-        for quad in range(4):
+        for quad in range(P // QUADRANT):
+            first = QUADRANT * quad
+            scale_rows = slice(PLANE_ROWS * quad, PLANE_ROWS * (quad + 1))
             nc.sync.dma_start(
-                out=w_planes[32 * quad : 32 * quad + 8, :].bitcast(I32),
-                in_=W_qk_scales[:, 4 * quad : 4 * quad + 4, :].bitcast(I32),
+                out=w_planes[first : first + G * PLANE_ROWS, :].bitcast(I32),
+                in_=W_qk_scales[:, scale_rows, :].bitcast(I32),
             )
             nc.sync.dma_start(
-                out=w_planes[32 * quad + 8 : 32 * quad + 16, 0:D].bitcast(I32),
-                in_=W_v_scales[:, 4 * quad : 4 * quad + 4, :].bitcast(I32),
+                out=w_planes[first + G * PLANE_ROWS : first + 2 * G * PLANE_ROWS, 0:D].bitcast(I32),
+                in_=W_v_scales[:, scale_rows, :].bitcast(I32),
             )
 
         wqk_words = consts.tile([P, G, 2 * D], I32, align_bytes=64)
@@ -78,10 +84,12 @@ def tile_relational_kernel(
         nc.scalar.dma_start(out=beta_bf[:], in_=beta.rearrange("(g p t) -> p g t", g=G, t=PACK))
         nc.scalar.dma_start(out=bqk_bf[:], in_=b_qk.rearrange("(n p t) -> p n t", n=QK_TILES, t=PACK))
 
-        bias_qk = consts.tile([P, 2 * D], BF16)
-        bias_v = consts.tile([P, D], BF16)
-        nc.sync.dma_start(out=bias_qk[:], in_=b_qk.partition_broadcast(P))
-        nc.sync.dma_start(out=bias_v[:], in_=b_v.partition_broadcast(P))
+        bias_rows = consts.tile([P, 3 * D], BF16)
+        nc.vector.memset(bias_rows[:].bitcast(I32), 0)
+        nc.scalar.dma_start(out=bias_rows[0:1, 0 : 2 * D], in_=b_qk.unsqueeze(0))
+        nc.scalar.dma_start(out=bias_rows[0:1, 2 * D : 3 * D], in_=b_v.unsqueeze(0))
+        ones = consts.tile([P, P], BF16)
+        nc.vector.memset(ones[:], 1.0)
 
         warm = consts.tile([P, 1], F32)
         nc.vector.memset(warm[:], 1.0)
@@ -126,20 +134,24 @@ def tile_relational_kernel(
                 op1=ALU.mult,
             )
             rows = x_in[b][:, m, :].rearrange("p (g q t) -> p g t q", g=G, t=PACK)
-            if b == 0 and m % 2 == 0:
-                nc.scalar.activation(
-                    out=y[b][:, m], in_=rows, func=ACT.Identity, scale=rstd[:, 0:1], bias=shift[:, 0:1]
-                )
-            else:
-                nc.gpsimd.tensor_scalar(
-                    out=y[b][:, m], in0=rows, scalar1=rstd[:, 0:1], scalar2=shift[:, 0:1], op0=ALU.mult, op1=ALU.add
-                )
+            nc.scalar.activation(
+                out=y[b][:, m, 0], in_=rows[:, 0], func=ACT.Identity, scale=rstd[:, 0:1], bias=shift[:, 0:1]
+            )
+            nc.gpsimd.tensor_scalar(
+                out=y[b][:, m, 1],
+                in0=rows[:, 1],
+                scalar1=rstd[:, 0:1],
+                scalar2=shift[:, 0:1],
+                op0=ALU.mult,
+                op1=ALU.add,
+            )
 
-        def normalise_tiles(first, last):
-            for i in range(first, last):
-                statistics(i // M_TILES, i % M_TILES)
-                if i > 0:
-                    normalise((i - 1) // M_TILES, (i - 1) % M_TILES)
+        def normalise_batch(b):
+            for m in range(M_TILES):
+                statistics(b, m)
+                if m > 0:
+                    normalise(b, m - 1)
+            normalise(b, M_TILES - 1)
 
         gamma_col = consts.tile([P, G * PACK], F32)
         beta_col = consts.tile([P, G * PACK], F32)
@@ -174,8 +186,8 @@ def tile_relational_kernel(
 
         def group_pass(b, g):
             nc.vector.tensor_copy(
-                out=x_grouped[b][:, g].rearrange("p (c i) t -> p c t i", i=4),
-                in_=x_planes[b][:, g].rearrange("p t (c i) -> p c t i", i=4),
+                out=x_grouped[b][:, g].rearrange("p (c i) t -> p c t i", i=RUN),
+                in_=x_planes[b][:, g].rearrange("p t (c i) -> p c t i", i=RUN),
             )
 
         def quantise_pass(b, g):
@@ -185,6 +197,25 @@ def tile_relational_kernel(
                 in_=x_grouped[b][:, g].rearrange("p c t -> p (c t)"),
             )
 
+        bias_q = consts.tile([P, D], F32)
+        bias_v = consts.tile([P, D], F32)
+
+        def spread_biases():
+            for n in range(QK_TILES + V_TILES):
+                spread = psum.tile([P, N_TILE], F32, name="bank")
+                nc.tensor.matmul(
+                    out=spread[:], lhsT=ones[:], rhs=bias_rows[:, n * N_TILE : (n + 1) * N_TILE], start=True, stop=True
+                )
+                if n < QK_TILES:
+                    nc.scalar.copy(
+                        out=bias_q[:, n * N_TILE // 2 : (n + 1) * N_TILE // 2],
+                        in_=spread[:].rearrange("p (f e) -> p f e", e=2)[:, :, 0],
+                    )
+                else:
+                    nc.scalar.copy(
+                        out=bias_v[:, (n - QK_TILES) * N_TILE : (n - QK_TILES + 1) * N_TILE], in_=spread[:]
+                    )
+
         def product(b, m, words, plane_start, cols):
             acc = psum.tile([P, N_TILE], F32, name="bank")
             for g in range(G):
@@ -193,7 +224,7 @@ def tile_relational_kernel(
                     lhsT=x_codes[b][:, g, m * P : (m + 1) * P].bitcast(FP8X4),
                     lhsT_scale=x_scales[b][:, g, m * P : (m + 1) * P],
                     rhs=words[:, g, cols].bitcast(FP8X4),
-                    rhs_scale=w_planes[plane_start + PACK * g : P, cols],
+                    rhs_scale=w_planes[plane_start + PLANE_ROWS * g : P, cols],
                     start=(g == 0),
                     stop=(g == G - 1),
                 )
@@ -203,14 +234,14 @@ def tile_relational_kernel(
 
         def project_qk(b, n):
             cols = slice(n * N_TILE, (n + 1) * N_TILE)
-            q_sb = results.tile([P, 4, M_TILES, HD], F32, name="q_sb")
+            q_sb = results.tile([P, QK_HEADS, M_TILES, HD], F32, name="q_sb")
             k_rows[(b, n)] = results.tile([P, M_TILES, 2, P], F32, name="k_rows")
             for m in range(M_TILES):
                 acc = product(b, m, wqk_words, 0, cols)
                 nc.vector.tensor_tensor(
                     out=q_sb[:, :, m, :],
-                    in0=acc[:].rearrange("p (h j e) -> p h j e", h=4, e=2)[:, :, :, 0],
-                    in1=bias_qk[:, cols].rearrange("p (h j e) -> p h j e", h=4, e=2)[:, :, :, 0],
+                    in0=acc[:].rearrange("p (h j e) -> p h j e", h=QK_HEADS, e=2)[:, :, :, 0],
+                    in1=bias_q[:, n * N_TILE // 2 : (n + 1) * N_TILE // 2].rearrange("p (h j) -> p h j", h=QK_HEADS),
                     op=ALU.add,
                 )
                 nc.scalar.copy(
@@ -218,7 +249,7 @@ def tile_relational_kernel(
                     in_=acc[:].rearrange("p (f c e) -> p c f e", c=2, e=2)[:, :, :, 1],
                 )
             nc.sync.dma_start(
-                out=out_0[b, 4 * n : 4 * n + 4].rearrange("h (p m) j -> p h (m j)", m=M_TILES),
+                out=out_0[b, QK_HEADS * n : QK_HEADS * (n + 1)].rearrange("h (p m) j -> p h (m j)", m=M_TILES),
                 in_=q_sb[:].rearrange("p h m j -> p h (m j)"),
             )
 
@@ -230,21 +261,12 @@ def tile_relational_kernel(
                 for m in range(M_TILES):
                     nc.tensor.transpose(out=banks[c][:, m, :], in_=k_rows[(b, n)][:, m, c, :], identity=ident[:])
             for c in range(2):
-                if c == 1 and b == B - 1:
-                    nc.vector.tensor_scalar(
-                        out=k_sb[:, c, :].rearrange("f (p m) -> f p m", m=M_TILES),
-                        in0=banks[c][:].rearrange("f m p -> f p m"),
-                        scalar1=bk_col[:, n, c : c + 1],
-                        scalar2=None,
-                        op0=ALU.add,
-                    )
-                else:
-                    nc.scalar.activation(
-                        out=k_sb[:, c, :].rearrange("f (p m) -> f p m", m=M_TILES),
-                        in_=banks[c][:].rearrange("f m p -> f p m"),
-                        func=ACT.Identity,
-                        bias=bk_col[:, n, c : c + 1],
-                    )
+                nc.scalar.activation(
+                    out=k_sb[:, c, :].rearrange("f (p m) -> f p m", m=M_TILES),
+                    in_=banks[c][:].rearrange("f m p -> f p m"),
+                    func=ACT.Identity,
+                    bias=bk_col[:, n, c : c + 1],
+                )
             features = out_1[b].rearrange("h j r -> (h j) r")[2 * P * n : 2 * P * (n + 1), :]
             nc.sync.dma_start(
                 out=features.rearrange("(f c) r -> f (c r)", c=2), in_=k_sb[:].rearrange("f c r -> f (c r)")
@@ -252,23 +274,21 @@ def tile_relational_kernel(
 
         def project_v(b, n):
             cols = slice(n * N_TILE, (n + 1) * N_TILE)
-            v_sb = results.tile([P, 8, M_TILES, HD], F32, name="v_sb")
+            v_sb = results.tile([P, V_HEADS, M_TILES, HD], F32, name="v_sb")
             for m in range(M_TILES):
-                acc = product(b, m, wv_words, 2 * PACK, cols)
+                acc = product(b, m, wv_words, G * PLANE_ROWS, cols)
                 nc.vector.tensor_tensor(
                     out=v_sb[:, :, m, :],
-                    in0=acc[:].rearrange("p (h j) -> p h j", h=8),
-                    in1=bias_v[:, cols].rearrange("p (h j) -> p h j", h=8),
+                    in0=acc[:].rearrange("p (h j) -> p h j", h=V_HEADS),
+                    in1=bias_v[:, cols].rearrange("p (h j) -> p h j", h=V_HEADS),
                     op=ALU.add,
                 )
-            for half in range(2):
-                heads = slice(4 * half, 4 * half + 4)
-                nc.sync.dma_start(
-                    out=out_2[b, 8 * n : 8 * n + 8][heads].rearrange("h (p m) j -> p h (m j)", m=M_TILES),
-                    in_=v_sb[:, heads].rearrange("p h m j -> p h (m j)"),
-                )
+            nc.sync.dma_start(
+                out=out_2[b, V_HEADS * n : V_HEADS * (n + 1)].rearrange("h (p m) j -> p h (m j)", m=M_TILES),
+                in_=v_sb[:].rearrange("p h m j -> p h (m j)"),
+            )
 
-        normalise_tiles(0, EARLY_TILES)
+        normalise_batch(0)
         nc.vector.tensor_copy(out=gamma_col[:], in_=gamma_bf[:].rearrange("p g t -> p (g t)"))
         nc.vector.tensor_copy(out=beta_col[:], in_=beta_bf[:].rearrange("p g t -> p (g t)"))
         nc.vector.tensor_copy(out=bk_col[:], in_=bqk_bf[:].rearrange("p n (c e) -> p n c e", e=2)[:, :, :, 1])
@@ -278,8 +298,8 @@ def tile_relational_kernel(
         quantise_pass(0, 0)
         group_pass(0, 1)
         quantise_pass(0, 1)
-        normalise_tiles(EARLY_TILES, B * M_TILES)
-        normalise(B - 1, M_TILES - 1)
+        spread_biases()
+        normalise_batch(1)
 
         for b in range(B):
             more = b + 1 < B

@@ -114,12 +114,8 @@ def tile_relational_kernel(
                 nc.vector.bn_stats(out=stats[:, s, :], in_=x_in[b][:, m, s * BN_CHUNK : (s + 1) * BN_CHUNK])
             mean_var[(b, m)] = small.tile([P, 2], F32, name="mean_var")
             nc.vector.bn_aggr(out=mean_var[(b, m)][:], in_=stats[:].rearrange("p s k -> p (s k)"))
-            var_eps = small.tile([P, 1], F32, name="var_eps")
-            nc.vector.tensor_scalar(
-                out=var_eps[:], in0=mean_var[(b, m)][:, 1:2], scalar1=LN_EPS, scalar2=None, op0=ALU.add
-            )
             std[(b, m)] = small.tile([P, 1], F32, name="std")
-            nc.scalar.activation(out=std[(b, m)][:], in_=var_eps[:], func=ACT.Sqrt)
+            nc.scalar.activation(out=std[(b, m)][:], in_=mean_var[(b, m)][:, 1:2], func=ACT.Sqrt, bias=LN_EPS)
 
         def normalise(b, m):
             rstd = small.tile([P, 1], F32, name="rstd")
@@ -216,19 +212,31 @@ def tile_relational_kernel(
                         out=bias_v[:, (n - QK_TILES) * N_TILE : (n - QK_TILES + 1) * N_TILE], in_=spread[:]
                     )
 
+        def one_pass(acc, g, b, m, words, plane_start, cols):
+            nc.tensor.matmul_mx(
+                out=acc,
+                lhsT=x_codes[b][:, g, m * P : (m + 1) * P].bitcast(FP8X4),
+                lhsT_scale=x_scales[b][:, g, m * P : (m + 1) * P],
+                rhs=words[:, g, cols].bitcast(FP8X4),
+                rhs_scale=w_planes[plane_start + PLANE_ROWS * g : P, cols],
+                start=(g == 0),
+                stop=(g == G - 1),
+            )
+
         def product(b, m, words, plane_start, cols):
-            acc = psum.tile([P, N_TILE], F32, name="bank")
+            bank = psum.tile([P, N_TILE], F32, name="bank")
+            acc = bank[:, 0 : cols.stop - cols.start]
             for g in range(G):
-                nc.tensor.matmul_mx(
-                    out=acc[:],
-                    lhsT=x_codes[b][:, g, m * P : (m + 1) * P].bitcast(FP8X4),
-                    lhsT_scale=x_scales[b][:, g, m * P : (m + 1) * P],
-                    rhs=words[:, g, cols].bitcast(FP8X4),
-                    rhs_scale=w_planes[plane_start + PLANE_ROWS * g : P, cols],
-                    start=(g == 0),
-                    stop=(g == G - 1),
-                )
+                one_pass(acc, g, b, m, words, plane_start, cols)
             return acc
+
+        opened = {}
+
+        def open_qk(b, n):
+            for m in range(M_TILES):
+                bank = psum.tile([P, N_TILE], F32, name="bank")
+                opened[(b, n, m)] = bank[:]
+                one_pass(opened[(b, n, m)], 0, b, m, wqk_words, 0, slice(n * N_TILE, (n + 1) * N_TILE))
 
         k_rows = {}
 
@@ -237,16 +245,20 @@ def tile_relational_kernel(
             q_sb = results.tile([P, QK_HEADS, M_TILES, HD], F32, name="q_sb")
             k_rows[(b, n)] = results.tile([P, M_TILES, 2, P], F32, name="k_rows")
             for m in range(M_TILES):
-                acc = product(b, m, wqk_words, 0, cols)
+                if (b, n, m) in opened:
+                    acc = opened[(b, n, m)]
+                    one_pass(acc, 1, b, m, wqk_words, 0, cols)
+                else:
+                    acc = product(b, m, wqk_words, 0, cols)
                 nc.vector.tensor_tensor(
                     out=q_sb[:, :, m, :],
-                    in0=acc[:].rearrange("p (h j e) -> p h j e", h=QK_HEADS, e=2)[:, :, :, 0],
+                    in0=acc.rearrange("p (h j e) -> p h j e", h=QK_HEADS, e=2)[:, :, :, 0],
                     in1=bias_q[:, n * N_TILE // 2 : (n + 1) * N_TILE // 2].rearrange("p (h j) -> p h j", h=QK_HEADS),
                     op=ALU.add,
                 )
                 nc.scalar.copy(
                     out=k_rows[(b, n)][:, m],
-                    in_=acc[:].rearrange("p (f c e) -> p c f e", c=2, e=2)[:, :, :, 1],
+                    in_=acc.rearrange("p (f c e) -> p c f e", c=2, e=2)[:, :, :, 1],
                 )
             nc.sync.dma_start(
                 out=out_0[b, QK_HEADS * n : QK_HEADS * (n + 1)].rearrange("h (p m) j -> p h (m j)", m=M_TILES),
@@ -272,19 +284,19 @@ def tile_relational_kernel(
                 out=features.rearrange("(f c) r -> f (c r)", c=2), in_=k_sb[:].rearrange("f c r -> f (c r)")
             )
 
-        def project_v(b, n):
-            cols = slice(n * N_TILE, (n + 1) * N_TILE)
-            v_sb = results.tile([P, V_HEADS, M_TILES, HD], F32, name="v_sb")
+        def project_v(b, first, width):
+            cols = slice(first, first + width)
+            v_sb = results.tile([P, width // HD, M_TILES, HD], F32, name="v_sb")
             for m in range(M_TILES):
                 acc = product(b, m, wv_words, G * PLANE_ROWS, cols)
                 nc.vector.tensor_tensor(
                     out=v_sb[:, :, m, :],
-                    in0=acc[:].rearrange("p (h j) -> p h j", h=V_HEADS),
-                    in1=bias_v[:, cols].rearrange("p (h j) -> p h j", h=V_HEADS),
+                    in0=acc.rearrange("p (h j) -> p h j", j=HD),
+                    in1=bias_v[:, cols].rearrange("p (h j) -> p h j", j=HD),
                     op=ALU.add,
                 )
             nc.sync.dma_start(
-                out=out_2[b, V_HEADS * n : V_HEADS * (n + 1)].rearrange("h (p m) j -> p h (m j)", m=M_TILES),
+                out=out_2[b, first // HD : (first + width) // HD].rearrange("h (p m) j -> p h (m j)", m=M_TILES),
                 in_=v_sb[:].rearrange("p h m j -> p h (m j)"),
             )
 
@@ -296,9 +308,11 @@ def tile_relational_kernel(
         group_pass(0, 0)
         transpose_pass(0, 1)
         quantise_pass(0, 0)
+        spread_biases()
+        open_qk(0, 0)
+        open_qk(0, 1)
         group_pass(0, 1)
         quantise_pass(0, 1)
-        spread_biases()
         normalise_batch(1)
 
         for b in range(B):
@@ -306,7 +320,7 @@ def tile_relational_kernel(
             project_qk(b, 0)
             project_qk(b, 1)
             transpose_k(b, 0)
-            project_v(b, 0)
+            project_v(b, 0, N_TILE)
             if more:
                 transpose_pass(b + 1, 0)
             transpose_k(b, 1)
@@ -321,5 +335,9 @@ def tile_relational_kernel(
             if more:
                 group_pass(b + 1, 1)
                 quantise_pass(b + 1, 1)
-            project_v(b, 1)
-            transpose_k(b, 3)
+                project_v(b, N_TILE, N_TILE)
+                transpose_k(b, 3)
+            else:
+                project_v(b, N_TILE, N_TILE // 2)
+                transpose_k(b, 3)
+                project_v(b, N_TILE + N_TILE // 2, N_TILE // 2)

@@ -70,11 +70,11 @@ def tile_relational_kernel(
         wv_words = consts.tile([P, G, D], I32, align_bytes=64)
         for g in range(G):
             nc.sync.dma_start(
-                out=wqk_words[:, g, :], in_=W_qk_words[g].rearrange("p n t -> p (n t)").bitcast(I32)
+                out=wv_words[:, g, :], in_=W_v_words[g].rearrange("p n t -> p (n t)").bitcast(I32)
             )
         for g in range(G):
             nc.sync.dma_start(
-                out=wv_words[:, g, :], in_=W_v_words[g].rearrange("p n t -> p (n t)").bitcast(I32)
+                out=wqk_words[:, g, :], in_=W_qk_words[g].rearrange("p n t -> p (n t)").bitcast(I32)
             )
 
         gamma_bf = consts.tile([P, G, PACK], BF16)
@@ -308,36 +308,36 @@ def tile_relational_kernel(
         group_pass(0, 0)
         transpose_pass(0, 1)
         quantise_pass(0, 0)
-        spread_biases()
-        open_qk(0, 0)
-        open_qk(0, 1)
         group_pass(0, 1)
         quantise_pass(0, 1)
+        spread_biases()
         normalise_batch(1)
 
-        for b in range(B):
-            more = b + 1 < B
-            project_qk(b, 0)
-            project_qk(b, 1)
-            transpose_k(b, 0)
-            project_v(b, 0, N_TILE)
-            if more:
-                transpose_pass(b + 1, 0)
-            transpose_k(b, 1)
-            project_qk(b, 2)
-            if more:
-                group_pass(b + 1, 0)
-                transpose_pass(b + 1, 1)
-            project_qk(b, 3)
-            if more:
-                quantise_pass(b + 1, 0)
-            transpose_k(b, 2)
-            if more:
-                group_pass(b + 1, 1)
-                quantise_pass(b + 1, 1)
-                project_v(b, N_TILE, N_TILE)
-                transpose_k(b, 3)
-            else:
-                project_v(b, N_TILE, N_TILE // 2)
-                transpose_k(b, 3)
-                project_v(b, N_TILE + N_TILE // 2, N_TILE // 2)
+        project_v(0, 0, N_TILE // 2)
+        project_v(0, N_TILE // 2, N_TILE // 2)
+        project_v(0, N_TILE, N_TILE)
+        project_qk(0, 0)
+        transpose_pass(1, 0)
+        project_qk(0, 1)
+        transpose_k(0, 0)
+        group_pass(1, 0)
+        transpose_pass(1, 1)
+        project_qk(0, 2)
+        quantise_pass(1, 0)
+        transpose_k(0, 1)
+        group_pass(1, 1)
+        quantise_pass(1, 1)
+        project_qk(0, 3)
+        transpose_k(0, 2)
+        project_qk(1, 0)
+        transpose_k(0, 3)
+        project_qk(1, 1)
+        transpose_k(1, 0)
+        project_v(1, 0, N_TILE)
+        transpose_k(1, 1)
+        project_qk(1, 2)
+        project_qk(1, 3)
+        transpose_k(1, 2)
+        project_v(1, N_TILE, N_TILE // 2)
+        transpose_k(1, 3)
+        project_v(1, N_TILE + N_TILE // 2, N_TILE // 2)

@@ -162,7 +162,7 @@ def tile_relational_kernel(
                     nc.tensor.transpose(out=banks[t][:, m, :], in_=y[b][:, m, g, t, :], identity=ident[:])
             for t in range(PACK):
                 col = g * PACK + t
-                if t % 2 == 0:
+                if t % 2 == 0 or b == 0 and g == 1 and t == 1:
                     nc.scalar.activation(
                         out=x_planes[b][:, g, t, :],
                         in_=banks[t][:].rearrange("p m n -> p (m n)"),
@@ -301,9 +301,9 @@ def tile_relational_kernel(
             )
 
         normalise_batch(0)
-        nc.vector.tensor_copy(out=gamma_col[:], in_=gamma_bf[:].rearrange("p g t -> p (g t)"))
-        nc.vector.tensor_copy(out=beta_col[:], in_=beta_bf[:].rearrange("p g t -> p (g t)"))
-        nc.vector.tensor_copy(out=bk_col[:], in_=bqk_bf[:].rearrange("p n (c e) -> p n c e", e=2)[:, :, :, 1])
+        nc.gpsimd.tensor_copy(out=gamma_col[:], in_=gamma_bf[:].rearrange("p g t -> p (g t)"))
+        nc.gpsimd.tensor_copy(out=beta_col[:], in_=beta_bf[:].rearrange("p g t -> p (g t)"))
+        nc.gpsimd.tensor_copy(out=bk_col[:], in_=bqk_bf[:].rearrange("p n (c e) -> p n c e", e=2)[:, :, :, 1])
         transpose_pass(0, 0)
         group_pass(0, 0)
         transpose_pass(0, 1)
@@ -312,9 +312,7 @@ def tile_relational_kernel(
         quantise_pass(0, 1)
         spread_biases()
         normalise_batch(1)
-
-        project_v(0, 0, N_TILE // 2)
-        project_v(0, N_TILE // 2, N_TILE // 2)
+        project_v(0, 0, N_TILE)
         project_v(0, N_TILE, N_TILE)
         project_qk(0, 0)
         transpose_pass(1, 0)

from contextlib import ExitStack

import concourse.mybir as mybir
from concourse.masks import make_identity

F32 = mybir.dt.float32
BF16 = mybir.dt.bfloat16
I32 = mybir.dt.int32
U8 = mybir.dt.uint8
FP8X4 = mybir.dt.float8_e4m3fn_x4
ACT = mybir.ActivationFunctionType
ALU = mybir.AluOpType

P = 128
QUADRANT = 32
PACK = 4
K_PASS = P * PACK
PLANE_ROWS = 4
N_TILE = 512
PSUM_BANKS = 8

B, NE, D, HD = 2, 512, 1024, 64
LN_EPS = 1e-5
M_TILES = NE // P
G = D // K_PASS
QK_TILES = 2 * D // N_TILE
V_TILES = D // N_TILE
QK_HEADS = N_TILE // (2 * HD)
V_HEADS = N_TILE // HD
BN_CHUNK = 512
BN_STATS = 6
RUN = 4

FLOPS = 2 * B * NE * D * 3 * D


def tile_relational_kernel(
    tc, inp, gamma, beta, W_qk_words, W_qk_scales, b_qk, W_v_words, W_v_scales, b_v, out_0, out_1, out_2
):
    nc = tc.nc
    with ExitStack() as ctx:
        consts = ctx.enter_context(tc.tile_pool(name="consts", bufs=1))
        batch = ctx.enter_context(tc.tile_pool(name="batch", bufs=B))
        small = ctx.enter_context(tc.tile_pool(name="small", bufs=B * M_TILES))
        results = ctx.enter_context(tc.tile_pool(name="results", bufs=4))
        psum = ctx.enter_context(tc.psum_pool(name="psum", bufs=PSUM_BANKS))

        x_in = []
        for b in range(B):
            x_in.append(batch.tile([P, M_TILES, D], BF16, name="x_in"))
            rows = inp[b].rearrange("(p m) d -> p m d", m=M_TILES)
            for m in range(M_TILES):
                nc.sync.dma_start(out=x_in[b][:, m, :], in_=rows[:, m, :])

        w_planes = consts.tile([P, 2 * D], U8, align_bytes=64)
        nc.vector.memset(w_planes[:].bitcast(I32), 0)
        for quad in range(P // QUADRANT):
            first = QUADRANT * quad
            scale_rows = slice(PLANE_ROWS * quad, PLANE_ROWS * (quad + 1))
            nc.sync.dma_start(
                out=w_planes[first : first + G * PLANE_ROWS, :].bitcast(I32),
                in_=W_qk_scales[:, scale_rows, :].bitcast(I32),
            )
            nc.sync.dma_start(
                out=w_planes[first + G * PLANE_ROWS : first + 2 * G * PLANE_ROWS, 0:D].bitcast(I32),
                in_=W_v_scales[:, scale_rows, :].bitcast(I32),
            )

        wqk_words = consts.tile([P, G, 2 * D], I32, align_bytes=64)
        wv_words = consts.tile([P, G, D], I32, align_bytes=64)
        for g in range(G):
            nc.sync.dma_start(
                out=wv_words[:, g, :], in_=W_v_words[g].rearrange("p n t -> p (n t)").bitcast(I32)
            )
        for g in range(G):
            nc.sync.dma_start(
                out=wqk_words[:, g, :], in_=W_qk_words[g].rearrange("p n t -> p (n t)").bitcast(I32)
            )

        gamma_bf = consts.tile([P, G, PACK], BF16)
        beta_bf = consts.tile([P, G, PACK], BF16)
        bqk_bf = consts.tile([P, QK_TILES, PACK], BF16)
        nc.scalar.dma_start(out=gamma_bf[:], in_=gamma.rearrange("(g p t) -> p g t", g=G, t=PACK))
        nc.scalar.dma_start(out=beta_bf[:], in_=beta.rearrange("(g p t) -> p g t", g=G, t=PACK))
        nc.scalar.dma_start(out=bqk_bf[:], in_=b_qk.rearrange("(n p t) -> p n t", n=QK_TILES, t=PACK))

        bias_rows = consts.tile([P, 3 * D], BF16)
        nc.vector.memset(bias_rows[:].bitcast(I32), 0)
        nc.scalar.dma_start(out=bias_rows[0:1, 0 : 2 * D], in_=b_qk.unsqueeze(0))
        nc.scalar.dma_start(out=bias_rows[0:1, 2 * D : 3 * D], in_=b_v.unsqueeze(0))
        ones = consts.tile([P, P], BF16)
        nc.vector.memset(ones[:], 1.0)

        warm = consts.tile([P, 1], F32)
        nc.vector.memset(warm[:], 1.0)
        nc.scalar.activation(out=warm[:], in_=warm[:], func=ACT.Sqrt)

        ident = consts.tile([P, P], F32)
        make_identity(nc, ident[:])

        y, x_planes, x_grouped, x_codes, x_scales = [], [], [], [], []
        for b in range(B):
            y.append(batch.tile([P, M_TILES, G, PACK, P], F32, name="y"))
            x_planes.append(batch.tile([P, G, PACK, NE], BF16, name="x_planes"))
            x_grouped.append(batch.tile([P, G, NE, PACK], BF16, name="x_grouped", align_bytes=64))
            x_codes.append(batch.tile([P, G, NE], I32, name="x_codes", align_bytes=64))
            x_scales.append(batch.tile([P, G, NE], U8, name="x_scales", align_bytes=64))

        mean_var, std = {}, {}

        def statistics(b, m):
            stats = small.tile([P, D // BN_CHUNK, BN_STATS], F32, name="stats")
            for s in range(D // BN_CHUNK):
                nc.vector.bn_stats(out=stats[:, s, :], in_=x_in[b][:, m, s * BN_CHUNK : (s + 1) * BN_CHUNK])
            mean_var[(b, m)] = small.tile([P, 2], F32, name="mean_var")
            nc.vector.bn_aggr(out=mean_var[(b, m)][:], in_=stats[:].rearrange("p s k -> p (s k)"))
            std[(b, m)] = small.tile([P, 1], F32, name="std")
            nc.scalar.activation(out=std[(b, m)][:], in_=mean_var[(b, m)][:, 1:2], func=ACT.Sqrt, bias=LN_EPS)

        def normalise(b, m):
            rstd = small.tile([P, 1], F32, name="rstd")
            nc.vector.reciprocal(out=rstd[:], in_=std[(b, m)][:])
            shift = small.tile([P, 1], F32, name="shift")
            nc.vector.tensor_scalar(
                out=shift[:],
                in0=mean_var[(b, m)][:, 0:1],
                scalar1=rstd[:, 0:1],
                scalar2=-1.0,
                op0=ALU.mult,
                op1=ALU.mult,
            )
            rows = x_in[b][:, m, :].rearrange("p (g q t) -> p g t q", g=G, t=PACK)
            nc.scalar.activation(
                out=y[b][:, m, 0], in_=rows[:, 0], func=ACT.Identity, scale=rstd[:, 0:1], bias=shift[:, 0:1]
            )
            nc.gpsimd.tensor_scalar(
                out=y[b][:, m, 1],
                in0=rows[:, 1],
                scalar1=rstd[:, 0:1],
                scalar2=shift[:, 0:1],
                op0=ALU.mult,
                op1=ALU.add,
            )

        def normalise_batch(b):
            for m in range(M_TILES):
                statistics(b, m)
                if m > 0:
                    normalise(b, m - 1)
            normalise(b, M_TILES - 1)

        gamma_col = consts.tile([P, G * PACK], F32)
        beta_col = consts.tile([P, G * PACK], F32)
        bk_col = consts.tile([P, QK_TILES, 2], F32)

        def transpose_pass(b, g):
            banks = []
            for t in range(PACK):
                banks.append(psum.tile([P, M_TILES, P], F32, name="bank"))
            for m in range(M_TILES):
                for t in range(PACK):
                    nc.tensor.transpose(out=banks[t][:, m, :], in_=y[b][:, m, g, t, :], identity=ident[:])
            for t in range(PACK):
                col = g * PACK + t
                if t % 2 == 0 or b == 0 and g == 1 and t == 1:
                    nc.scalar.activation(
                        out=x_planes[b][:, g, t, :],
                        in_=banks[t][:].rearrange("p m n -> p (m n)"),
                        func=ACT.Identity,
                        scale=gamma_col[:, col : col + 1],
                        bias=beta_col[:, col : col + 1],
                    )
                else:
                    nc.vector.tensor_scalar(
                        out=x_planes[b][:, g, t, :],
                        in0=banks[t][:].rearrange("p m n -> p (m n)"),
                        scalar1=gamma_col[:, col : col + 1],
                        scalar2=beta_col[:, col : col + 1],
                        op0=ALU.mult,
                        op1=ALU.add,
                    )

        def group_pass(b, g):
            nc.vector.tensor_copy(
                out=x_grouped[b][:, g].rearrange("p (c i) t -> p c t i", i=RUN),
                in_=x_planes[b][:, g].rearrange("p t (c i) -> p c t i", i=RUN),
            )

        def quantise_pass(b, g):
            nc.vector.quantize_mx(
                out=x_codes[b][:, g, :].bitcast(FP8X4),
                scales=x_scales[b][:, g, :],
                in_=x_grouped[b][:, g].rearrange("p c t -> p (c t)"),
            )

        bias_q = consts.tile([P, D], F32)
        bias_v = consts.tile([P, D], F32)

        def spread_biases():
            for n in range(QK_TILES + V_TILES):
                spread = psum.tile([P, N_TILE], F32, name="bank")
                nc.tensor.matmul(
                    out=spread[:], lhsT=ones[:], rhs=bias_rows[:, n * N_TILE : (n + 1) * N_TILE], start=True, stop=True
                )
                if n < QK_TILES:
                    nc.scalar.copy(
                        out=bias_q[:, n * N_TILE // 2 : (n + 1) * N_TILE // 2],
                        in_=spread[:].rearrange("p (f e) -> p f e", e=2)[:, :, 0],
                    )
                else:
                    nc.scalar.copy(
                        out=bias_v[:, (n - QK_TILES) * N_TILE : (n - QK_TILES + 1) * N_TILE], in_=spread[:]
                    )

        def one_pass(acc, g, b, m, words, plane_start, cols):
            nc.tensor.matmul_mx(
                out=acc,
                lhsT=x_codes[b][:, g, m * P : (m + 1) * P].bitcast(FP8X4),
                lhsT_scale=x_scales[b][:, g, m * P : (m + 1) * P],
                rhs=words[:, g, cols].bitcast(FP8X4),
                rhs_scale=w_planes[plane_start + PLANE_ROWS * g : P, cols],
                start=(g == 0),
                stop=(g == G - 1),
            )

        def product(b, m, words, plane_start, cols):
            bank = psum.tile([P, N_TILE], F32, name="bank")
            acc = bank[:, 0 : cols.stop - cols.start]
            for g in range(G):
                one_pass(acc, g, b, m, words, plane_start, cols)
            return acc

        opened = {}

        def open_qk(b, n):
            for m in range(M_TILES):
                bank = psum.tile([P, N_TILE], F32, name="bank")
                opened[(b, n, m)] = bank[:]
                one_pass(opened[(b, n, m)], 0, b, m, wqk_words, 0, slice(n * N_TILE, (n + 1) * N_TILE))

        k_rows = {}

        def project_qk(b, n):
            cols = slice(n * N_TILE, (n + 1) * N_TILE)
            q_sb = results.tile([P, QK_HEADS, M_TILES, HD], F32, name="q_sb")
            k_rows[(b, n)] = results.tile([P, M_TILES, 2, P], F32, name="k_rows")
            for m in range(M_TILES):
                if (b, n, m) in opened:
                    acc = opened[(b, n, m)]
                    one_pass(acc, 1, b, m, wqk_words, 0, cols)
                else:
                    acc = product(b, m, wqk_words, 0, cols)
                nc.vector.tensor_tensor(
                    out=q_sb[:, :, m, :],
                    in0=acc.rearrange("p (h j e) -> p h j e", h=QK_HEADS, e=2)[:, :, :, 0],
                    in1=bias_q[:, n * N_TILE // 2 : (n + 1) * N_TILE // 2].rearrange("p (h j) -> p h j", h=QK_HEADS),
                    op=ALU.add,
                )
                nc.scalar.copy(
                    out=k_rows[(b, n)][:, m],
                    in_=acc.rearrange("p (f c e) -> p c f e", c=2, e=2)[:, :, :, 1],
                )
            nc.sync.dma_start(
                out=out_0[b, QK_HEADS * n : QK_HEADS * (n + 1)].rearrange("h (p m) j -> p h (m j)", m=M_TILES),
                in_=q_sb[:].rearrange("p h m j -> p h (m j)"),
            )

        def transpose_k(b, n):
            k_sb = results.tile([P, 2, NE], F32, name="k_sb")
            banks = []
            for c in range(2):
                banks.append(psum.tile([P, M_TILES, P], F32, name="bank"))
                for m in range(M_TILES):
                    nc.tensor.transpose(out=banks[c][:, m, :], in_=k_rows[(b, n)][:, m, c, :], identity=ident[:])
            for c in range(2):
                nc.scalar.activation(
                    out=k_sb[:, c, :].rearrange("f (p m) -> f p m", m=M_TILES),
                    in_=banks[c][:].rearrange("f m p -> f p m"),
                    func=ACT.Identity,
                    bias=bk_col[:, n, c : c + 1],
                )
            features = out_1[b].rearrange("h j r -> (h j) r")[2 * P * n : 2 * P * (n + 1), :]
            nc.sync.dma_start(
                out=features.rearrange("(f c) r -> f (c r)", c=2), in_=k_sb[:].rearrange("f c r -> f (c r)")
            )

        def project_v(b, first, width):
            cols = slice(first, first + width)
            v_sb = results.tile([P, width // HD, M_TILES, HD], F32, name="v_sb")
            for m in range(M_TILES):
                acc = product(b, m, wv_words, G * PLANE_ROWS, cols)
                nc.vector.tensor_tensor(
                    out=v_sb[:, :, m, :],
                    in0=acc.rearrange("p (h j) -> p h j", j=HD),
                    in1=bias_v[:, cols].rearrange("p (h j) -> p h j", j=HD),
                    op=ALU.add,
                )
            nc.sync.dma_start(
                out=out_2[b, first // HD : (first + width) // HD].rearrange("h (p m) j -> p h (m j)", m=M_TILES),
                in_=v_sb[:].rearrange("p h m j -> p h (m j)"),
            )

        normalise_batch(0)
        nc.gpsimd.tensor_copy(out=gamma_col[:], in_=gamma_bf[:].rearrange("p g t -> p (g t)"))
        nc.gpsimd.tensor_copy(out=beta_col[:], in_=beta_bf[:].rearrange("p g t -> p (g t)"))
        nc.gpsimd.tensor_copy(out=bk_col[:], in_=bqk_bf[:].rearrange("p n (c e) -> p n c e", e=2)[:, :, :, 1])
        transpose_pass(0, 0)
        group_pass(0, 0)
        transpose_pass(0, 1)
        quantise_pass(0, 0)
        group_pass(0, 1)
        quantise_pass(0, 1)
        spread_biases()
        normalise_batch(1)
        project_v(0, 0, N_TILE)
        project_v(0, N_TILE, N_TILE)
        project_qk(0, 0)
        transpose_pass(1, 0)
        project_qk(0, 1)
        transpose_k(0, 0)
        group_pass(1, 0)
        transpose_pass(1, 1)
        project_qk(0, 2)
        quantise_pass(1, 0)
        transpose_k(0, 1)
        group_pass(1, 1)
        quantise_pass(1, 1)
        project_qk(0, 3)
        transpose_k(0, 2)
        project_qk(1, 0)
        transpose_k(0, 3)
        project_qk(1, 1)
        transpose_k(1, 0)
        project_v(1, 0, N_TILE)
        transpose_k(1, 1)
        project_qk(1, 2)
        project_qk(1, 3)
        transpose_k(1, 2)
        project_v(1, N_TILE, N_TILE // 2)
        transpose_k(1, 3)
        project_v(1, N_TILE + N_TILE // 2, N_TILE // 2)
